import numpy as np
import ml_dtypes


def mxq(x, axis, fmt="e4m3"):
    dtype, down = {"e4m3": (ml_dtypes.float8_e4m3fn, 7), "e5m2": (ml_dtypes.float8_e5m2, 14)}[fmt]
    v = np.moveaxis(np.asarray(x, np.float32).astype(ml_dtypes.bfloat16).astype(np.float64), axis, -1)
    blocks = v.reshape(v.shape[:-1] + (-1, 32))
    amax = np.abs(blocks).max(-1, keepdims=True)
    byte = np.maximum(np.where(amax > 0, np.frexp(amax)[1] - 1 + 127, 0) - down, 1)
    scale = np.exp2(byte - 127.0)
    codes = (blocks / scale).astype(np.float32).astype(dtype).astype(np.float64)
    return np.moveaxis((codes * scale).reshape(v.shape), -1, axis)


WIDE = False


def mx_kscale(k):
    if not WIDE:
        return np.ones(k)
    levels = np.array([10, -10, 5, -5, 0])
    if k % 512:
        return np.exp2(np.random.permutation(np.resize(levels, k // 32))).repeat(32)
    a = np.empty((k // 512, 16))
    for p in range(k // 512):
        a[p, :8] = np.random.permutation(np.resize(levels, 8))
        for g in range(8):
            far = levels[np.abs(levels - a[p, g]) >= 10]
            a[p, g + 8] = far[np.random.randint(len(far))]
    return np.exp2(a.ravel()).repeat(32)


BF16 = ml_dtypes.bfloat16


def bf(x):
    return np.asarray(x, np.float32).astype(BF16)


def f64(x):
    return np.asarray(x).astype(np.float64)


B, T, I, H = 128, 8, 1024, 1024


def sigmoid(v):
    return 1.0 / (1.0 + np.exp(-v))


def setup_inputs():
    s = mx_kscale(I)
    d = {"x": bf(np.random.standard_normal((B, T, I)) * s),
         "h0": bf(np.random.standard_normal((B, H))),
         "c0": bf(np.random.standard_normal((B, H)))}
    for n in ("f", "i", "g"):
        d["W_" + n] = bf(np.random.standard_normal((H, I)) / np.sqrt(I) / s)
        d["b_" + n] = bf(np.random.standard_normal(H) * 0.5)
        d["R_" + n] = bf(np.random.standard_normal((H, H)) / np.sqrt(H))
        d["rb_" + n] = bf(np.random.standard_normal(H) * 0.5)
    return d


def reference(x, h0, c0, W_f, b_f, R_f, rb_f, W_i, b_i, R_i, rb_i, W_g, b_g, R_g, rb_g):
    xq = mxq(f64(x), 2, "e4m3")
    h0v = f64(h0)

    def pre(W, b, R, rb):
        return (xq @ mxq(f64(W), 1, "e4m3").T) + f64(b) + (h0v @ f64(R).T + f64(rb))[:, None, :]

    ft = sigmoid(pre(W_f, b_f, R_f, rb_f))
    it = sigmoid(pre(W_i, b_i, R_i, rb_i))
    gt = np.tanh(pre(W_g, b_g, R_g, rb_g))
    c = ft * f64(c0)[:, None, :] + it * gt
    h_seq = np.tanh(c)
    hidden_seq = np.transpose(h_seq, (1, 0, 2)).reshape(T * B, H).T
    return (hidden_seq, h_seq[:, -1, :], c[:, -1, :])

@@ -1,0 +1,343 @@
+from contextlib import ExitStack
+
+import concourse.mybir as mybir
+from concourse.masks import make_identity
+
+F32 = mybir.dt.float32
+BF16 = mybir.dt.bfloat16
+U32 = mybir.dt.uint32
+U8 = mybir.dt.uint8
+FP8X4 = mybir.dt.float8_e4m3fn_x4
+ACT = mybir.ActivationFunctionType
+ALU = mybir.AluOpType
+
+P = 128
+BATCH, STEPS, FEATURES, HIDDEN = 128, 8, 1024, 1024
+GATES = 3
+ROW_TILES = HIDDEN // P
+WORD_BLOCKS = FEATURES // (2 * P)
+PASSES = FEATURES // (4 * P)
+HALF_STEPS = STEPS // 2
+HALF = HALF_STEPS * BATCH
+TOKENS = STEPS * BATCH
+LOAD_AHEAD = 4
+
+FLOPS = 2 * TOKENS * FEATURES * HIDDEN * GATES + 2 * BATCH * HIDDEN * HIDDEN * GATES
+
+
+def tile_lstm_cell_pa_kernel(
+    tc, x, h0, c0, W_f, b_f, R_f, rb_f, W_i, b_i, R_i, rb_i, W_g, b_g, R_g, rb_g, out_0, out_1, out_2
+):
+    nc = tc.nc
+    w_dram = (W_f, W_i, W_g)
+    r_dram = (R_f, R_i, R_g)
+    bias_dram = (b_f, rb_f, b_i, rb_i, b_g, rb_g)
+    gate_func = (ACT.Sigmoid, ACT.Sigmoid, ACT.Tanh)
+
+    with ExitStack() as ctx:
+        const = ctx.enter_context(tc.tile_pool(name="const", bufs=1))
+        raw_pool = ctx.enter_context(tc.tile_pool(name="raw", bufs=2 * GATES * LOAD_AHEAD))
+        stage = ctx.enter_context(tc.tile_pool(name="stage", bufs=6))
+        work = ctx.enter_context(tc.tile_pool(name="work", bufs=3))
+        keep = ctx.enter_context(tc.tile_pool(name="keep", bufs=ROW_TILES))
+        flip_psum = ctx.enter_context(tc.psum_pool(name="flip_psum", bufs=3))
+        rec_psum = ctx.enter_context(tc.psum_pool(name="rec_psum", bufs=1))
+        acc_psum = ctx.enter_context(tc.psum_pool(name="acc_psum", bufs=GATES))
+        c0_psum = ctx.enter_context(tc.psum_pool(name="c0_psum", bufs=1))
+
+        ctx.enter_context(tc.manual_schedule())
+
+        ident_f32 = const.tile([P, P], F32)
+        make_identity(nc, ident_f32[:])
+        ident_bf16 = const.tile([P, P], BF16)
+        make_identity(nc, ident_bf16[:])
+
+        bias_rows = const.tile([P, P], BF16)
+        nc.vector.memset(bias_rows[:], 0.0)
+        for v, vector in enumerate(bias_dram):
+            nc.scalar.dma_start(
+                out=bias_rows[v * ROW_TILES : (v + 1) * ROW_TILES, :],
+                in_=vector.rearrange("(jt p) -> jt p", p=P),
+            )
+
+        table_warmer = const.tile([P, 1], F32)
+        nc.vector.memset(table_warmer[:], 0.0)
+        nc.scalar.activation(out=table_warmer[:], in_=table_warmer[:], func=ACT.Sigmoid)
+
+        x_raw = const.tile([P, STEPS, FEATURES], BF16)
+        h0_raw = const.tile([P, HIDDEN], BF16)
+        c0_raw = const.tile([P, HIDDEN], BF16)
+
+        def load_x(first_step):
+            steps = slice(first_step, first_step + 2)
+            nc.sync.dma_start(out=x_raw[:, steps, :], in_=x[:, steps, :])
+
+        def load_rows(matrix, jt, name):
+            raw = raw_pool.tile([P, FEATURES], BF16, tag="raw", name=name)
+            nc.sync.dma_start(out=raw[:], in_=matrix[jt * P : (jt + 1) * P, :])
+            return raw
+
+        def load_r(jt):
+            r_raw[jt] = [load_rows(r_dram[n], jt, "r_raw") for n in range(GATES)]
+
+        def load_w(jt):
+            w_raw[jt] = [load_rows(w_dram[n], jt, "w_raw") for n in range(GATES)]
+
+        r_raw = {}
+        w_raw = {}
+        nc.sync.dma_start(out=h0_raw[:], in_=h0)
+        load_r(0)
+        load_x(4)
+        load_x(6)
+        load_w(0)
+        nc.sync.dma_start(out=c0_raw[:], in_=c0)
+        load_r(1)
+        load_x(0)
+        load_x(2)
+        load_w(1)
+        for jt in range(2, LOAD_AHEAD):
+            load_r(jt)
+            load_w(jt)
+
+        def transpose_words(rows_bf16, borrow=False, for_mx=False):
+            words = rows_bf16.bitcast(F32)
+            if borrow:
+                bank = acc_psum.tile([P, WORD_BLOCKS, P], F32, tag="acc", name="bank")
+            else:
+                bank = flip_psum.tile([P, WORD_BLOCKS, P], F32, tag="flip", name="bank")
+            for q in range(WORD_BLOCKS):
+                if for_mx:
+                    first = (q // 2) * 2 * P + q % 2
+                    block = words[:, first : first + 2 * P - 1 : 2]
+                else:
+                    block = words[:, q * P : (q + 1) * P]
+                nc.tensor.transpose(bank[:, q, :], block, ident_f32[:])
+            return bank
+
+        def by_pass(bank):
+            return bank[:].rearrange("p (c u) n -> p c n u", u=2)
+
+        def leave_psum(n, out, in_):
+            if n % GATES == 1:
+                nc.vector.tensor_copy(out=out, in_=in_)
+            else:
+                nc.scalar.copy(out=out, in_=in_)
+
+        x_grouped = const.tile([P, PASSES, 4 * TOKENS], BF16, align_bytes=64)
+        x_codes = const.tile([P, PASSES, TOKENS], U32, align_bytes=64)
+        x_scales = const.tile([P, PASSES, TOKENS], U8, align_bytes=64)
+        x_grouped_words = x_grouped[:].bitcast(F32).rearrange("p c (n u) -> p c n u", u=2)
+
+        def prepare_x(half):
+            for t in range(half * HALF_STEPS, (half + 1) * HALF_STEPS):
+                bank = transpose_words(x_raw[:, t, :], borrow=(t % 2 == 1), for_mx=True)
+                columns = x_grouped_words[:, :, t * BATCH : (t + 1) * BATCH, :]
+                if t % 2 == 0:
+                    nc.scalar.copy(out=columns, in_=by_pass(bank))
+                else:
+                    nc.vector.tensor_copy(out=columns, in_=by_pass(bank))
+            for c in range(PASSES):
+                nc.vector.quantize_mx(
+                    out=x_codes[:, c, half * HALF : (half + 1) * HALF].bitcast(FP8X4),
+                    scales=x_scales[:, c, half * HALF : (half + 1) * HALF],
+                    in_=x_grouped[:, c, half * 4 * HALF : (half + 1) * 4 * HALF],
+                )
+
+        h0T = const.tile([P, WORD_BLOCKS, BATCH, 2], BF16)
+
+        def prepare_h0():
+            bank = transpose_words(h0_raw[:])
+            nc.vector.tensor_copy(
+                out=h0T[:].rearrange("p q b e -> p (q b e)").bitcast(F32),
+                in_=bank[:].rearrange("p q b -> p (q b)"),
+            )
+
+        r_T = {}
+        rec_sums = {}
+        rec = {}
+        w_grouped = {}
+        w_mx = {}
+
+        def transpose_r(jt, prologue=False):
+            if jt >= ROW_TILES:
+                return
+            r_T[jt] = []
+            for n in range(GATES):
+                bank = transpose_words(r_raw[jt][n][:], borrow=(prologue and n % 2 == 1))
+                flipped = stage.tile([P, WORD_BLOCKS, P, 2], BF16, tag="r_T", name="r_T")
+                nc.scalar.copy(
+                    out=flipped[:].rearrange("p q j e -> p (q j e)").bitcast(F32),
+                    in_=bank[:].rearrange("p q j -> p (q j)"),
+                )
+                r_T[jt].append(flipped)
+
+        rec_steps = [(n, q, e) for n in range(GATES) for q in range(WORD_BLOCKS) for e in range(2)]
+
+        def recurrent_matmuls(jt, part):
+            if jt >= ROW_TILES:
+                return
+            if part == 0:
+                rec_sums[jt] = rec_psum.tile([P, GATES, BATCH], F32, tag="rec", name="rec_sums")
+            count = len(rec_steps) // 2
+            for n, q, e in rec_steps[part * count : (part + 1) * count]:
+                nc.tensor.matmul(
+                    out=rec_sums[jt][:, n, :],
+                    lhsT=r_T[jt][n][:, q, :, e],
+                    rhs=h0T[:, q, :, e],
+                    start=(q == 0 and e == 0),
+                    stop=(q == WORD_BLOCKS - 1 and e == 1),
+                )
+            if part == 1:
+                rec[jt] = work.tile([P, GATES, BATCH], F32, tag="rec_sb", name="rec")
+                nc.vector.tensor_copy(out=rec[jt][:], in_=rec_sums[jt][:])
+
+        def transpose_w(jt, prologue=False):
+            if jt >= ROW_TILES:
+                return
+            w_grouped[jt] = []
+            for n in range(GATES):
+                bank = transpose_words(w_raw[jt][n][:], borrow=(prologue and n % 2 == 1), for_mx=True)
+                values = stage.tile([P, 4 * PASSES * P], BF16, tag="w_grouped", name="w_grouped", align_bytes=64)
+                leave_psum(
+                    n,
+                    out=values[:].bitcast(F32).rearrange("p (c j u) -> p c j u", c=PASSES, u=2),
+                    in_=by_pass(bank),
+                )
+                w_grouped[jt].append(values)
+
+        def quantise_w(jt):
+            if jt >= ROW_TILES:
+                return
+            w_mx[jt] = []
+            for n in range(GATES):
+                codes = stage.tile([P, PASSES, P], U32, tag="w_codes", name="w_codes", align_bytes=64)
+                scales = stage.tile([P, PASSES, P], U8, tag="w_scales", name="w_scales", align_bytes=64)
+                nc.vector.quantize_mx(
+                    out=codes[:].rearrange("p c j -> p (c j)").bitcast(FP8X4),
+                    scales=scales[:].rearrange("p c j -> p (c j)"),
+                    in_=w_grouped[jt][n][:],
+                )
+                w_mx[jt].append((codes, scales))
+
+        def gates(jt, half):
+            tokens = slice(half * HALF, (half + 1) * HALF)
+            gate_tiles = []
+            for n in range(GATES):
+                codes, scales = w_mx[jt][n]
+                acc = acc_psum.tile([P, HALF_STEPS, BATCH], F32, tag="acc", name="acc")
+                for c in range(PASSES):
+                    nc.tensor.matmul_mx(
+                        out=acc[:].rearrange("p t b -> p (t b)"),
+                        lhsT=codes[:, c, :].bitcast(FP8X4),
+                        lhsT_scale=scales[:, c, :],
+                        rhs=x_codes[:, c, tokens].bitcast(FP8X4),
+                        rhs_scale=x_scales[:, c, tokens],
+                        start=(c == 0),
+                        stop=(c == PASSES - 1),
+                    )
+                gate = work.tile([P, HALF_STEPS, BATCH], F32, tag="gate%d" % n, name="gate")
+                nc.vector.tensor_tensor(
+                    out=gate[:],
+                    in0=acc[:],
+                    in1=rec[jt][:, n, :].unsqueeze(1).to_broadcast([P, HALF_STEPS, BATCH]),
+                    op=ALU.add,
+                )
+                nc.scalar.activation(out=gate[:], in_=gate[:], func=gate_func[n], bias=bias[:, n, jt : jt + 1])
+                gate_tiles.append(gate)
+            return gate_tiles
+
+        def kept_state(jt, half, gate_tiles):
+            f_gate = gate_tiles[0]
+            nc.vector.tensor_tensor(
+                out=f_gate[:],
+                in0=f_gate[:],
+                in1=c0T[:, jt, :].unsqueeze(1).to_broadcast([P, HALF_STEPS, BATCH]),
+                op=ALU.mult,
+            )
+
+        def new_state(jt, half, gate_tiles):
+            f_gate, i_gate, g_gate = gate_tiles
+            engine = nc.vector if jt == ROW_TILES - 1 else nc.gpsimd
+            engine.tensor_tensor(out=i_gate[:], in0=i_gate[:], in1=g_gate[:], op=ALU.mult)
+            c_new = (keep if half == 1 else work).tile([P, HALF_STEPS, BATCH], F32, tag="c_new", name="c_new")
+            engine.tensor_tensor(out=c_new[:], in0=f_gate[:], in1=i_gate[:], op=ALU.add)
+            return c_new
+
+        def finish(jt, half, c_new):
+            h_new = (keep if half == 1 else work).tile([P, HALF_STEPS, BATCH], F32, tag="h_new", name="h_new")
+            nc.scalar.activation(out=h_new[:], in_=c_new[:], func=ACT.Tanh)
+            nc.sync.dma_start(
+                out=out_0[jt * P : (jt + 1) * P, half * HALF : (half + 1) * HALF],
+                in_=h_new[:].rearrange("p t b -> p (t b)"),
+            )
+            if half == 1:
+                last_tiles[jt] = (h_new, c_new)
+
+        last_tiles = {}
+        last_sb = const.tile([P, 2, HIDDEN], F32)
+
+        def store_last(first):
+            columns = slice(first * P, (first + WORD_BLOCKS) * P)
+            for which, out_last in enumerate((out_1, out_2)):
+                bank = flip_psum.tile([P, WORD_BLOCKS, P], F32, tag="flip", name="last_bank")
+                for q in range(WORD_BLOCKS):
+                    nc.tensor.transpose(bank[:, q, :], last_tiles[first + q][which][:, HALF_STEPS - 1, :], ident_f32[:])
+                leave_psum(which, out=last_sb[:, which, columns], in_=bank[:].rearrange("p q j -> p (q j)"))
+                nc.sync.dma_start(out=out_last[:, columns], in_=last_sb[:, which, columns])
+
+        prepare_h0()
+        transpose_r(0, prologue=True)
+        prepare_x(1)
+        recurrent_matmuls(0, 0)
+        recurrent_matmuls(0, 1)
+        transpose_w(0, prologue=True)
+
+        bias_psum = flip_psum.tile([P, P], BF16, tag="flip", name="bias_psum")
+        nc.tensor.transpose(bias_psum[:], bias_rows[:], ident_bf16[:])
+        bias_pairs = const.tile([P, GATES, 2, ROW_TILES], F32)
+        nc.vector.tensor_copy(
+            out=bias_pairs[:],
+            in_=bias_psum[:, 0 : 2 * GATES * ROW_TILES].rearrange("p (n s jt) -> p n s jt", n=GATES, s=2),
+        )
+        bias = const.tile([P, GATES, ROW_TILES], F32)
+        nc.vector.tensor_tensor(out=bias[:], in0=bias_pairs[:, :, 0, :], in1=bias_pairs[:, :, 1, :], op=ALU.add)
+
+        c0T = c0_psum.tile([P, ROW_TILES, BATCH], BF16, tag="c0T", name="c0T")
+        for jt in range(ROW_TILES):
+            nc.tensor.transpose(c0T[:, jt, :], c0_raw[:, jt * P : (jt + 1) * P], ident_bf16[:])
+
+        quantise_w(0)
+        transpose_r(1, prologue=True)
+        prepare_x(0)
+        transpose_w(1, prologue=True)
+
+        gated = None
+        updated = None
+        for jt in range(ROW_TILES):
+            if jt + LOAD_AHEAD < ROW_TILES:
+                load_r(jt + LOAD_AHEAD)
+                load_w(jt + LOAD_AHEAD)
+            for half in (1, 0):
+                gate_tiles = gates(jt, half)
+                before = updated
+                if gated is not None:
+                    kept_state(*gated)
+                if half == 1:
+                    quantise_w(jt + 1)
+                if gated is not None:
+                    updated = (gated[0], gated[1], new_state(*gated))
+                gated = (jt, half, gate_tiles)
+                if half == 1:
+                    recurrent_matmuls(jt + 1, 0)
+                    transpose_r(jt + 2)
+                else:
+                    recurrent_matmuls(jt + 1, 1)
+                    transpose_w(jt + 2)
+                if before is not None:
+                    finish(*before)
+            if jt == ROW_TILES - 2:
+                store_last(0)
+        finish(*updated)
+        kept_state(*gated)
+        finish(gated[0], gated[1], new_state(*gated))
+        store_last(WORD_BLOCKS)

@@ -219,15 +219,15 @@ def tile_lstm_cell_pa_kernel(
                 )
                 w_mx[jt].append((codes, scales))
 
-        def gates(jt, half):
-            tokens = slice(half * HALF, (half + 1) * HALF)
+        def gates(jt, first, count):
+            tokens = slice(first * BATCH, (first + count) * BATCH)
             gate_tiles = []
             for n in range(GATES):
                 codes, scales = w_mx[jt][n]
                 acc = acc_psum.tile([P, HALF_STEPS, BATCH], F32, tag="acc", name="acc")
                 for c in range(PASSES):
                     nc.tensor.matmul_mx(
-                        out=acc[:].rearrange("p t b -> p (t b)"),
+                        out=acc[:, 0:count, :].rearrange("p t b -> p (t b)"),
                         lhsT=codes[:, c, :].bitcast(FP8X4),
                         lhsT_scale=scales[:, c, :],
                         rhs=x_codes[:, c, tokens].bitcast(FP8X4),
@@ -235,54 +235,60 @@ def tile_lstm_cell_pa_kernel(
                         start=(c == 0),
                         stop=(c == PASSES - 1),
                     )
-                gate = work.tile([P, HALF_STEPS, BATCH], F32, tag="gate%d" % n, name="gate")
+                gate = work.tile([P, count, BATCH], F32, tag="gate%d" % n, name="gate")
                 nc.vector.tensor_tensor(
                     out=gate[:],
-                    in0=acc[:],
-                    in1=rec[jt][:, n, :].unsqueeze(1).to_broadcast([P, HALF_STEPS, BATCH]),
+                    in0=acc[:, 0:count, :],
+                    in1=rec[jt][:, n, :].unsqueeze(1).to_broadcast([P, count, BATCH]),
                     op=ALU.add,
                 )
                 nc.scalar.activation(out=gate[:], in_=gate[:], func=gate_func[n], bias=bias[:, n, jt : jt + 1])
                 gate_tiles.append(gate)
             return gate_tiles
 
-        def kept_state(jt, half, gate_tiles):
+        def kept_state(step, gate_tiles):
+            jt, first, count = step
             f_gate = gate_tiles[0]
             nc.vector.tensor_tensor(
                 out=f_gate[:],
                 in0=f_gate[:],
-                in1=c0T[:, jt, :].unsqueeze(1).to_broadcast([P, HALF_STEPS, BATCH]),
+                in1=c0T[:, jt, :].unsqueeze(1).to_broadcast([P, count, BATCH]),
                 op=ALU.mult,
             )
 
-        def new_state(jt, half, gate_tiles):
+        def has_last_time_step(step):
+            return step[1] + step[2] == STEPS
+
+        def new_state(step, gate_tiles, engine):
             f_gate, i_gate, g_gate = gate_tiles
-            engine = nc.vector if jt == ROW_TILES - 1 else nc.gpsimd
             engine.tensor_tensor(out=i_gate[:], in0=i_gate[:], in1=g_gate[:], op=ALU.mult)
-            c_new = (keep if half == 1 else work).tile([P, HALF_STEPS, BATCH], F32, tag="c_new", name="c_new")
+            pool = keep if has_last_time_step(step) else work
+            c_new = pool.tile([P, step[2], BATCH], F32, tag="c_new", name="c_new")
             engine.tensor_tensor(out=c_new[:], in0=f_gate[:], in1=i_gate[:], op=ALU.add)
             return c_new
 
-        def finish(jt, half, c_new):
-            h_new = (keep if half == 1 else work).tile([P, HALF_STEPS, BATCH], F32, tag="h_new", name="h_new")
+        def finish(step, c_new):
+            jt, first, count = step
+            pool = keep if has_last_time_step(step) else work
+            h_new = pool.tile([P, count, BATCH], F32, tag="h_new", name="h_new")
             nc.scalar.activation(out=h_new[:], in_=c_new[:], func=ACT.Tanh)
             nc.sync.dma_start(
-                out=out_0[jt * P : (jt + 1) * P, half * HALF : (half + 1) * HALF],
+                out=out_0[jt * P : (jt + 1) * P, first * BATCH : (first + count) * BATCH],
                 in_=h_new[:].rearrange("p t b -> p (t b)"),
             )
-            if half == 1:
-                last_tiles[jt] = (h_new, c_new)
+            if has_last_time_step(step):
+                last_tiles[jt] = (h_new[:, count - 1, :], c_new[:, count - 1, :])
 
         last_tiles = {}
         last_sb = const.tile([P, 2, HIDDEN], F32)
 
-        def store_last(first):
-            columns = slice(first * P, (first + WORD_BLOCKS) * P)
+        def store_last(first, count):
+            columns = slice(first * P, (first + count) * P)
             for which, out_last in enumerate((out_1, out_2)):
                 bank = flip_psum.tile([P, WORD_BLOCKS, P], F32, tag="flip", name="last_bank")
-                for q in range(WORD_BLOCKS):
-                    nc.tensor.transpose(bank[:, q, :], last_tiles[first + q][which][:, HALF_STEPS - 1, :], ident_f32[:])
-                leave_psum(which, out=last_sb[:, which, columns], in_=bank[:].rearrange("p q j -> p (q j)"))
+                for q in range(count):
+                    nc.tensor.transpose(bank[:, q, :], last_tiles[first + q][which], ident_f32[:])
+                leave_psum(which, out=last_sb[:, which, columns], in_=bank[:, 0:count, :].rearrange("p q j -> p (q j)"))
                 nc.sync.dma_start(out=out_last[:, columns], in_=last_sb[:, which, columns])
 
         prepare_h0()
@@ -311,33 +317,38 @@ def tile_lstm_cell_pa_kernel(
         prepare_x(0)
         transpose_w(1, prologue=True)
 
+        steps = [(jt, first, HALF_STEPS) for jt in range(ROW_TILES - 1) for first in (HALF_STEPS, 0)]
+        steps += [(ROW_TILES - 1, first, HALF_STEPS // 2) for first in (4, 6, 0, 2)]
         gated = None
         updated = None
-        for jt in range(ROW_TILES):
-            if jt + LOAD_AHEAD < ROW_TILES:
+        for step in steps:
+            jt, first, count = step
+            opens_row_tile = first == HALF_STEPS
+            if opens_row_tile and jt + LOAD_AHEAD < ROW_TILES:
                 load_r(jt + LOAD_AHEAD)
                 load_w(jt + LOAD_AHEAD)
-            for half in (1, 0):
-                gate_tiles = gates(jt, half)
-                before = updated
-                if gated is not None:
-                    kept_state(*gated)
-                if half == 1:
-                    quantise_w(jt + 1)
-                if gated is not None:
-                    updated = (gated[0], gated[1], new_state(*gated))
-                gated = (jt, half, gate_tiles)
-                if half == 1:
-                    recurrent_matmuls(jt + 1, 0)
-                    transpose_r(jt + 2)
-                else:
-                    recurrent_matmuls(jt + 1, 1)
-                    transpose_w(jt + 2)
-                if before is not None:
-                    finish(*before)
-            if jt == ROW_TILES - 2:
-                store_last(0)
+            gate_tiles = gates(*step)
+            before = updated
+            if gated is not None:
+                kept_state(*gated)
+            if opens_row_tile:
+                quantise_w(jt + 1)
+            if gated is not None:
+                updated = (gated[0], new_state(*gated, nc.gpsimd))
+            gated = (step, gate_tiles)
+            if opens_row_tile:
+                recurrent_matmuls(jt + 1, 0)
+                transpose_r(jt + 2)
+            elif first == 0:
+                recurrent_matmuls(jt + 1, 1)
+                transpose_w(jt + 2)
+            if before is not None:
+                finish(*before)
+            if step == (ROW_TILES - 2, 0, HALF_STEPS):
+                store_last(0, WORD_BLOCKS)
+            if step == (ROW_TILES - 1, 6, HALF_STEPS // 2):
+                store_last(WORD_BLOCKS, 3)
         finish(*updated)
         kept_state(*gated)
-        finish(gated[0], gated[1], new_state(*gated))
-        store_last(WORD_BLOCKS)
+        finish(gated[0], new_state(*gated, nc.vector))
+        store_last(ROW_TILES - 1, 1)

@@ -20,6 +20,7 @@ PASSES = FEATURES // (4 * P)
 HALF_STEPS = STEPS // 2
 HALF = HALF_STEPS * BATCH
 TOKENS = STEPS * BATCH
+RUN = 8
 LOAD_AHEAD = 4
 
 FLOPS = 2 * TOKENS * FEATURES * HIDDEN * GATES + 2 * BATCH * HIDDEN * HIDDEN * GATES
@@ -38,6 +39,7 @@ def tile_lstm_cell_pa_kernel(
         const = ctx.enter_context(tc.tile_pool(name="const", bufs=1))
         raw_pool = ctx.enter_context(tc.tile_pool(name="raw", bufs=2 * GATES * LOAD_AHEAD))
         stage = ctx.enter_context(tc.tile_pool(name="stage", bufs=6))
+        order_pool = ctx.enter_context(tc.tile_pool(name="order", bufs=9))
         work = ctx.enter_context(tc.tile_pool(name="work", bufs=3))
         keep = ctx.enter_context(tc.tile_pool(name="keep", bufs=ROW_TILES))
         flip_psum = ctx.enter_context(tc.psum_pool(name="flip_psum", bufs=3))
@@ -47,6 +49,10 @@ def tile_lstm_cell_pa_kernel(
 
         ctx.enter_context(tc.manual_schedule())
 
+        table_warmer = const.tile([P, 1], F32)
+        nc.vector.memset(table_warmer[:], 0.0)
+        nc.scalar.activation(out=table_warmer[:], in_=table_warmer[:], func=ACT.Sigmoid)
+
         ident_f32 = const.tile([P, P], F32)
         make_identity(nc, ident_f32[:])
         ident_bf16 = const.tile([P, P], BF16)
@@ -54,15 +60,6 @@ def tile_lstm_cell_pa_kernel(
 
         bias_rows = const.tile([P, P], BF16)
         nc.vector.memset(bias_rows[:], 0.0)
-        for v, vector in enumerate(bias_dram):
-            nc.scalar.dma_start(
-                out=bias_rows[v * ROW_TILES : (v + 1) * ROW_TILES, :],
-                in_=vector.rearrange("(jt p) -> jt p", p=P),
-            )
-
-        table_warmer = const.tile([P, 1], F32)
-        nc.vector.memset(table_warmer[:], 0.0)
-        nc.scalar.activation(out=table_warmer[:], in_=table_warmer[:], func=ACT.Sigmoid)
 
         x_raw = const.tile([P, STEPS, FEATURES], BF16)
         h0_raw = const.tile([P, HIDDEN], BF16)
@@ -78,40 +75,57 @@ def tile_lstm_cell_pa_kernel(
             return raw
 
         def load_r(jt):
-            r_raw[jt] = [load_rows(r_dram[n], jt, "r_raw") for n in range(GATES)]
+            if jt < ROW_TILES:
+                r_raw[jt] = [load_rows(r_dram[n], jt, "r_raw") for n in range(GATES)]
+
+        def load_bias(v):
+            nc.sync.dma_start(
+                out=bias_rows[v * ROW_TILES : (v + 1) * ROW_TILES, :],
+                in_=bias_dram[v].rearrange("(jt p) -> jt p", p=P),
+            )
 
         def load_w(jt):
-            w_raw[jt] = [load_rows(w_dram[n], jt, "w_raw") for n in range(GATES)]
+            if jt < ROW_TILES:
+                w_raw[jt] = [load_rows(w_dram[n], jt, "w_raw") for n in range(GATES)]
 
         r_raw = {}
         w_raw = {}
         nc.sync.dma_start(out=h0_raw[:], in_=h0)
         load_r(0)
         load_x(4)
+        load_bias(0)
         load_x(6)
+        load_bias(1)
         load_w(0)
-        nc.sync.dma_start(out=c0_raw[:], in_=c0)
+        load_bias(2)
         load_r(1)
+        load_bias(3)
         load_x(0)
+        load_bias(4)
         load_x(2)
+        load_bias(5)
+        nc.sync.dma_start(out=c0_raw[:], in_=c0)
         load_w(1)
         for jt in range(2, LOAD_AHEAD):
             load_r(jt)
             load_w(jt)
 
-        def transpose_words(rows_bf16, borrow=False, for_mx=False):
+        def order_words(rows_bf16, tag):
+            ordered = order_pool.tile([P, FEATURES], BF16, tag=tag, name="ordered")
+            nc.vector.tensor_copy(
+                out=ordered[:].bitcast(F32).rearrange("p (c u s r) -> p c u s r", c=PASSES, u=2, r=RUN),
+                in_=rows_bf16.bitcast(F32).rearrange("p (c s u r) -> p c u s r", c=PASSES, u=2, r=RUN),
+            )
+            return ordered[:]
+
+        def transpose_words(rows_bf16, borrow=False):
             words = rows_bf16.bitcast(F32)
             if borrow:
                 bank = acc_psum.tile([P, WORD_BLOCKS, P], F32, tag="acc", name="bank")
             else:
                 bank = flip_psum.tile([P, WORD_BLOCKS, P], F32, tag="flip", name="bank")
             for q in range(WORD_BLOCKS):
-                if for_mx:
-                    first = (q // 2) * 2 * P + q % 2
-                    block = words[:, first : first + 2 * P - 1 : 2]
-                else:
-                    block = words[:, q * P : (q + 1) * P]
-                nc.tensor.transpose(bank[:, q, :], block, ident_f32[:])
+                nc.tensor.transpose(bank[:, q, :], words[:, q * P : (q + 1) * P], ident_f32[:])
             return bank
 
         def by_pass(bank):
@@ -128,14 +142,21 @@ def tile_lstm_cell_pa_kernel(
         x_scales = const.tile([P, PASSES, TOKENS], U8, align_bytes=64)
         x_grouped_words = x_grouped[:].bitcast(F32).rearrange("p c (n u) -> p c n u", u=2)
 
-        def prepare_x(half):
+        x_ordered = {}
+
+        def order_x(t):
+            x_ordered[t] = order_words(x_raw[:, t, :], "ordered")
+
+        def transpose_x(half, borrow):
             for t in range(half * HALF_STEPS, (half + 1) * HALF_STEPS):
-                bank = transpose_words(x_raw[:, t, :], borrow=(t % 2 == 1), for_mx=True)
+                bank = transpose_words(x_ordered[t], borrow=(borrow and t % 2 == 1))
                 columns = x_grouped_words[:, :, t * BATCH : (t + 1) * BATCH, :]
                 if t % 2 == 0:
                     nc.scalar.copy(out=columns, in_=by_pass(bank))
                 else:
                     nc.vector.tensor_copy(out=columns, in_=by_pass(bank))
+
+        def quantise_x(half):
             for c in range(PASSES):
                 nc.vector.quantize_mx(
                     out=x_codes[:, c, half * HALF : (half + 1) * HALF].bitcast(FP8X4),
@@ -155,15 +176,16 @@ def tile_lstm_cell_pa_kernel(
         r_T = {}
         rec_sums = {}
         rec = {}
+        w_ordered = {}
         w_grouped = {}
         w_mx = {}
 
-        def transpose_r(jt, prologue=False):
+        def transpose_r(jt, borrow=False):
             if jt >= ROW_TILES:
                 return
             r_T[jt] = []
             for n in range(GATES):
-                bank = transpose_words(r_raw[jt][n][:], borrow=(prologue and n % 2 == 1))
+                bank = transpose_words(r_raw[jt][n][:], borrow=(borrow and n % 2 == 1))
                 flipped = stage.tile([P, WORD_BLOCKS, P, 2], BF16, tag="r_T", name="r_T")
                 nc.scalar.copy(
                     out=flipped[:].rearrange("p q j e -> p (q j e)").bitcast(F32),
@@ -191,12 +213,16 @@ def tile_lstm_cell_pa_kernel(
                 rec[jt] = work.tile([P, GATES, BATCH], F32, tag="rec_sb", name="rec")
                 nc.vector.tensor_copy(out=rec[jt][:], in_=rec_sums[jt][:])
 
-        def transpose_w(jt, prologue=False):
+        def order_w(jt):
+            if jt < ROW_TILES:
+                w_ordered[jt] = [order_words(w_raw[jt][n][:], "ordered") for n in range(GATES)]
+
+        def transpose_w(jt, borrow=False):
             if jt >= ROW_TILES:
                 return
             w_grouped[jt] = []
             for n in range(GATES):
-                bank = transpose_words(w_raw[jt][n][:], borrow=(prologue and n % 2 == 1), for_mx=True)
+                bank = transpose_words(w_ordered[jt][n], borrow=(borrow and n % 2 == 1))
                 values = stage.tile([P, 4 * PASSES * P], BF16, tag="w_grouped", name="w_grouped", align_bytes=64)
                 leave_psum(
                     n,
@@ -219,7 +245,8 @@ def tile_lstm_cell_pa_kernel(
                 )
                 w_mx[jt].append((codes, scales))
 
-        def gates(jt, first, count):
+        def gates(step):
+            jt, first, count = step
             tokens = slice(first * BATCH, (first + count) * BATCH)
             gate_tiles = []
             for n in range(GATES):
@@ -291,31 +318,46 @@ def tile_lstm_cell_pa_kernel(
                 leave_psum(which, out=last_sb[:, which, columns], in_=bank[:, 0:count, :].rearrange("p q j -> p (q j)"))
                 nc.sync.dma_start(out=out_last[:, columns], in_=last_sb[:, which, columns])
 
+        bias_pairs = const.tile([P, GATES, 2, ROW_TILES], F32)
+        bias = const.tile([P, GATES, ROW_TILES], F32)
+        c0T = c0_psum.tile([P, ROW_TILES, BATCH], BF16, tag="c0T", name="c0T")
+
+        def prepare_bias():
+            bias_psum = flip_psum.tile([P, P], BF16, tag="flip", name="bias_psum")
+            nc.tensor.transpose(bias_psum[:], bias_rows[:], ident_bf16[:])
+            nc.vector.tensor_copy(
+                out=bias_pairs[:],
+                in_=bias_psum[:, 0 : 2 * GATES * ROW_TILES].rearrange("p (n s jt) -> p n s jt", n=GATES, s=2),
+            )
+
+        def add_bias():
+            nc.vector.tensor_tensor(out=bias[:], in0=bias_pairs[:, :, 0, :], in1=bias_pairs[:, :, 1, :], op=ALU.add)
+
+        def transpose_c0():
+            for tile in range(ROW_TILES):
+                nc.tensor.transpose(c0T[:, tile, :], c0_raw[:, tile * P : (tile + 1) * P], ident_bf16[:])
+
+
         prepare_h0()
-        transpose_r(0, prologue=True)
-        prepare_x(1)
+        transpose_r(0, borrow=True)
+        for t in range(HALF_STEPS, STEPS): order_x(t)
+        transpose_x(1, borrow=True)
+        order_w(0)
+        quantise_x(1)
         recurrent_matmuls(0, 0)
         recurrent_matmuls(0, 1)
-        transpose_w(0, prologue=True)
-
-        bias_psum = flip_psum.tile([P, P], BF16, tag="flip", name="bias_psum")
-        nc.tensor.transpose(bias_psum[:], bias_rows[:], ident_bf16[:])
-        bias_pairs = const.tile([P, GATES, 2, ROW_TILES], F32)
-        nc.vector.tensor_copy(
-            out=bias_pairs[:],
-            in_=bias_psum[:, 0 : 2 * GATES * ROW_TILES].rearrange("p (n s jt) -> p n s jt", n=GATES, s=2),
-        )
-        bias = const.tile([P, GATES, ROW_TILES], F32)
-        nc.vector.tensor_tensor(out=bias[:], in0=bias_pairs[:, :, 0, :], in1=bias_pairs[:, :, 1, :], op=ALU.add)
-
-        c0T = c0_psum.tile([P, ROW_TILES, BATCH], BF16, tag="c0T", name="c0T")
-        for jt in range(ROW_TILES):
-            nc.tensor.transpose(c0T[:, jt, :], c0_raw[:, jt * P : (jt + 1) * P], ident_bf16[:])
-
+        transpose_w(0, borrow=True)
+        prepare_bias()
+        add_bias()
+        transpose_c0()
         quantise_w(0)
-        transpose_r(1, prologue=True)
-        prepare_x(0)
-        transpose_w(1, prologue=True)
+        for t in range(HALF_STEPS): order_x(t)
+        transpose_r(1, borrow=True)
+        order_w(1)
+        transpose_x(0, borrow=True)
+        quantise_x(0)
+        transpose_w(1, borrow=True)
+        order_w(2)
 
         steps = [(jt, first, HALF_STEPS) for jt in range(ROW_TILES - 1) for first in (HALF_STEPS, 0)]
         steps += [(ROW_TILES - 1, first, HALF_STEPS // 2) for first in (4, 6, 0, 2)]
@@ -324,22 +366,37 @@ def tile_lstm_cell_pa_kernel(
         for step in steps:
             jt, first, count = step
             opens_row_tile = first == HALF_STEPS
-            if opens_row_tile and jt + LOAD_AHEAD < ROW_TILES:
+            closes_row_tile = first == 0
+            if opens_row_tile:
                 load_r(jt + LOAD_AHEAD)
                 load_w(jt + LOAD_AHEAD)
-            gate_tiles = gates(*step)
+            gate_tiles = gates(step)
             before = updated
+            if jt == 0 and opens_row_tile:
+                quantise_w(1)
+                order_w(3)
+            elif jt == 0:
+                pass
+            elif opens_row_tile:
+                quantise_w(jt + 1)
+                order_w(jt + 3)
+            elif closes_row_tile:
+                pass
             if gated is not None:
                 kept_state(*gated)
-            if opens_row_tile:
-                quantise_w(jt + 1)
             if gated is not None:
                 updated = (gated[0], new_state(*gated, nc.gpsimd))
             gated = (step, gate_tiles)
-            if opens_row_tile:
+            if jt == 0 and opens_row_tile:
+                recurrent_matmuls(1, 0)
+                transpose_r(2)
+            elif jt == 0:
+                recurrent_matmuls(1, 1)
+                transpose_w(2)
+            elif opens_row_tile:
                 recurrent_matmuls(jt + 1, 0)
                 transpose_r(jt + 2)
-            elif first == 0:
+            elif closes_row_tile:
                 recurrent_matmuls(jt + 1, 1)
                 transpose_w(jt + 2)
             if before is not None:

@@ -21,6 +21,8 @@ HALF_STEPS = STEPS // 2
 HALF = HALF_STEPS * BATCH
 TOKENS = STEPS * BATCH
 RUN = 8
+R_ON_VECTOR = ()
+W_ON_VECTOR = (0, 1)
 LOAD_AHEAD = 4
 
 FLOPS = 2 * TOKENS * FEATURES * HIDDEN * GATES + 2 * BATCH * HIDDEN * HIDDEN * GATES
@@ -33,7 +35,6 @@ def tile_lstm_cell_pa_kernel(
     w_dram = (W_f, W_i, W_g)
     r_dram = (R_f, R_i, R_g)
     bias_dram = (b_f, rb_f, b_i, rb_i, b_g, rb_g)
-    gate_func = (ACT.Sigmoid, ACT.Sigmoid, ACT.Tanh)
 
     with ExitStack() as ctx:
         const = ctx.enter_context(tc.tile_pool(name="const", bufs=1))
@@ -92,20 +93,20 @@ def tile_lstm_cell_pa_kernel(
         w_raw = {}
         nc.sync.dma_start(out=h0_raw[:], in_=h0)
         load_r(0)
-        load_x(4)
         load_bias(0)
-        load_x(6)
         load_bias(1)
-        load_w(0)
+        load_x(4)
         load_bias(2)
-        load_r(1)
         load_bias(3)
-        load_x(0)
+        load_x(6)
         load_bias(4)
-        load_x(2)
         load_bias(5)
-        nc.sync.dma_start(out=c0_raw[:], in_=c0)
+        load_w(0)
+        load_r(1)
+        load_x(0)
+        load_x(2)
         load_w(1)
+        nc.sync.dma_start(out=c0_raw[:], in_=c0)
         for jt in range(2, LOAD_AHEAD):
             load_r(jt)
             load_w(jt)
@@ -131,8 +132,8 @@ def tile_lstm_cell_pa_kernel(
         def by_pass(bank):
             return bank[:].rearrange("p (c u) n -> p c n u", u=2)
 
-        def leave_psum(n, out, in_):
-            if n % GATES == 1:
+        def leave_psum(on_vector, out, in_):
+            if on_vector:
                 nc.vector.tensor_copy(out=out, in_=in_)
             else:
                 nc.scalar.copy(out=out, in_=in_)
@@ -147,14 +148,13 @@ def tile_lstm_cell_pa_kernel(
         def order_x(t):
             x_ordered[t] = order_words(x_raw[:, t, :], "ordered")
 
-        def transpose_x(half, borrow):
-            for t in range(half * HALF_STEPS, (half + 1) * HALF_STEPS):
-                bank = transpose_words(x_ordered[t], borrow=(borrow and t % 2 == 1))
-                columns = x_grouped_words[:, :, t * BATCH : (t + 1) * BATCH, :]
-                if t % 2 == 0:
-                    nc.scalar.copy(out=columns, in_=by_pass(bank))
-                else:
-                    nc.vector.tensor_copy(out=columns, in_=by_pass(bank))
+        def transpose_x(t, on_vector, borrow=False):
+            bank = transpose_words(x_ordered[t], borrow=borrow)
+            columns = x_grouped_words[:, :, t * BATCH : (t + 1) * BATCH, :]
+            if on_vector:
+                nc.vector.tensor_copy(out=columns, in_=by_pass(bank))
+            else:
+                nc.scalar.copy(out=columns, in_=by_pass(bank))
 
         def quantise_x(half):
             for c in range(PASSES):
@@ -187,7 +187,8 @@ def tile_lstm_cell_pa_kernel(
             for n in range(GATES):
                 bank = transpose_words(r_raw[jt][n][:], borrow=(borrow and n % 2 == 1))
                 flipped = stage.tile([P, WORD_BLOCKS, P, 2], BF16, tag="r_T", name="r_T")
-                nc.scalar.copy(
+                leave_psum(
+                    n in R_ON_VECTOR,
                     out=flipped[:].rearrange("p q j e -> p (q j e)").bitcast(F32),
                     in_=bank[:].rearrange("p q j -> p (q j)"),
                 )
@@ -211,13 +212,18 @@ def tile_lstm_cell_pa_kernel(
                 )
             if part == 1:
                 rec[jt] = work.tile([P, GATES, BATCH], F32, tag="rec_sb", name="rec")
-                nc.vector.tensor_copy(out=rec[jt][:], in_=rec_sums[jt][:])
+                nc.vector.tensor_tensor(
+                    out=rec[jt][:],
+                    in0=rec_sums[jt][:],
+                    in1=bias[:, :, jt].unsqueeze(2).to_broadcast([P, GATES, BATCH]),
+                    op=ALU.add,
+                )
 
         def order_w(jt):
             if jt < ROW_TILES:
                 w_ordered[jt] = [order_words(w_raw[jt][n][:], "ordered") for n in range(GATES)]
 
-        def transpose_w(jt, borrow=False):
+        def transpose_w(jt, borrow=False, on_vector=W_ON_VECTOR):
             if jt >= ROW_TILES:
                 return
             w_grouped[jt] = []
@@ -225,7 +231,7 @@ def tile_lstm_cell_pa_kernel(
                 bank = transpose_words(w_ordered[jt][n], borrow=(borrow and n % 2 == 1))
                 values = stage.tile([P, 4 * PASSES * P], BF16, tag="w_grouped", name="w_grouped", align_bytes=64)
                 leave_psum(
-                    n,
+                    n in on_vector,
                     out=values[:].bitcast(F32).rearrange("p (c j u) -> p c j u", c=PASSES, u=2),
                     in_=by_pass(bank),
                 )
@@ -248,7 +254,8 @@ def tile_lstm_cell_pa_kernel(
         def gates(step):
             jt, first, count = step
             tokens = slice(first * BATCH, (first + count) * BATCH)
-            gate_tiles = []
+            fi = work.tile([P, 2, count, BATCH], F32, tag="fi", name="fi")
+            g = work.tile([P, 1, count, BATCH], F32, tag="g", name="g")
             for n in range(GATES):
                 codes, scales = w_mx[jt][n]
                 acc = acc_psum.tile([P, HALF_STEPS, BATCH], F32, tag="acc", name="acc")
@@ -262,23 +269,23 @@ def tile_lstm_cell_pa_kernel(
                         start=(c == 0),
                         stop=(c == PASSES - 1),
                     )
-                gate = work.tile([P, count, BATCH], F32, tag="gate%d" % n, name="gate")
+                gate = (fi if n < 2 else g)[:, n % 2]
                 nc.vector.tensor_tensor(
-                    out=gate[:],
+                    out=gate,
                     in0=acc[:, 0:count, :],
                     in1=rec[jt][:, n, :].unsqueeze(1).to_broadcast([P, count, BATCH]),
                     op=ALU.add,
                 )
-                nc.scalar.activation(out=gate[:], in_=gate[:], func=gate_func[n], bias=bias[:, n, jt : jt + 1])
-                gate_tiles.append(gate)
-            return gate_tiles
+            nc.scalar.activation(out=fi[:], in_=fi[:], func=ACT.Sigmoid)
+            nc.scalar.activation(out=g[:], in_=g[:], func=ACT.Tanh)
+            return fi[:, 0], fi[:, 1], g[:, 0]
 
         def kept_state(step, gate_tiles):
             jt, first, count = step
             f_gate = gate_tiles[0]
             nc.vector.tensor_tensor(
-                out=f_gate[:],
-                in0=f_gate[:],
+                out=f_gate,
+                in0=f_gate,
                 in1=c0T[:, jt, :].unsqueeze(1).to_broadcast([P, count, BATCH]),
                 op=ALU.mult,
             )
@@ -288,10 +295,10 @@ def tile_lstm_cell_pa_kernel(
 
         def new_state(step, gate_tiles, engine):
             f_gate, i_gate, g_gate = gate_tiles
-            engine.tensor_tensor(out=i_gate[:], in0=i_gate[:], in1=g_gate[:], op=ALU.mult)
+            engine.tensor_tensor(out=i_gate, in0=i_gate, in1=g_gate, op=ALU.mult)
             pool = keep if has_last_time_step(step) else work
             c_new = pool.tile([P, step[2], BATCH], F32, tag="c_new", name="c_new")
-            engine.tensor_tensor(out=c_new[:], in0=f_gate[:], in1=i_gate[:], op=ALU.add)
+            engine.tensor_tensor(out=c_new[:], in0=f_gate, in1=i_gate, op=ALU.add)
             return c_new
 
         def finish(step, c_new):
@@ -315,7 +322,7 @@ def tile_lstm_cell_pa_kernel(
                 bank = flip_psum.tile([P, WORD_BLOCKS, P], F32, tag="flip", name="last_bank")
                 for q in range(count):
                     nc.tensor.transpose(bank[:, q, :], last_tiles[first + q][which], ident_f32[:])
-                leave_psum(which, out=last_sb[:, which, columns], in_=bank[:, 0:count, :].rearrange("p q j -> p (q j)"))
+                leave_psum(which == 1, out=last_sb[:, which, columns], in_=bank[:, 0:count, :].rearrange("p q j -> p (q j)"))
                 nc.sync.dma_start(out=out_last[:, columns], in_=last_sb[:, which, columns])
 
         bias_pairs = const.tile([P, GATES, 2, ROW_TILES], F32)
@@ -341,22 +348,28 @@ def tile_lstm_cell_pa_kernel(
         prepare_h0()
         transpose_r(0, borrow=True)
         for t in range(HALF_STEPS, STEPS): order_x(t)
-        transpose_x(1, borrow=True)
+        transpose_x(4, False)
+        transpose_x(5, True, borrow=True)
+        transpose_x(6, False)
+        transpose_x(7, False, borrow=True)
         order_w(0)
-        quantise_x(1)
         recurrent_matmuls(0, 0)
-        recurrent_matmuls(0, 1)
-        transpose_w(0, borrow=True)
         prepare_bias()
         add_bias()
-        transpose_c0()
-        quantise_w(0)
+        quantise_x(1)
+        transpose_w(0, borrow=True, on_vector=(2,))
+        recurrent_matmuls(0, 1)
         for t in range(HALF_STEPS): order_x(t)
-        transpose_r(1, borrow=True)
+        quantise_w(0)
+        transpose_r(1)
         order_w(1)
-        transpose_x(0, borrow=True)
+        transpose_x(0, False, borrow=True)
+        transpose_x(1, True)
+        transpose_x(2, False, borrow=True)
+        transpose_x(3, False)
         quantise_x(0)
-        transpose_w(1, borrow=True)
+        transpose_w(1, on_vector=())
+        transpose_c0()
         order_w(2)
 
         steps = [(jt, first, HALF_STEPS) for jt in range(ROW_TILES - 1) for first in (HALF_STEPS, 0)]

@@ -41,7 +41,7 @@ def tile_lstm_cell_pa_kernel(
         raw_pool = ctx.enter_context(tc.tile_pool(name="raw", bufs=2 * GATES * LOAD_AHEAD))
         stage = ctx.enter_context(tc.tile_pool(name="stage", bufs=6))
         order_pool = ctx.enter_context(tc.tile_pool(name="order", bufs=9))
-        work = ctx.enter_context(tc.tile_pool(name="work", bufs=3))
+        work = ctx.enter_context(tc.tile_pool(name="work", bufs=4))
         keep = ctx.enter_context(tc.tile_pool(name="keep", bufs=ROW_TILES))
         flip_psum = ctx.enter_context(tc.psum_pool(name="flip_psum", bufs=3))
         rec_psum = ctx.enter_context(tc.psum_pool(name="rec_psum", bufs=1))
@@ -105,8 +105,8 @@ def tile_lstm_cell_pa_kernel(
         load_r(1)
         load_x(0)
         load_x(2)
-        load_w(1)
         nc.sync.dma_start(out=c0_raw[:], in_=c0)
+        load_w(1)
         for jt in range(2, LOAD_AHEAD):
             load_r(jt)
             load_w(jt)
@@ -347,13 +347,13 @@ def tile_lstm_cell_pa_kernel(
 
         prepare_h0()
         transpose_r(0, borrow=True)
+        recurrent_matmuls(0, 0)
         for t in range(HALF_STEPS, STEPS): order_x(t)
         transpose_x(4, False)
         transpose_x(5, True, borrow=True)
         transpose_x(6, False)
         transpose_x(7, False, borrow=True)
         order_w(0)
-        recurrent_matmuls(0, 0)
         prepare_bias()
         add_bias()
         quantise_x(1)
@@ -362,14 +362,14 @@ def tile_lstm_cell_pa_kernel(
         for t in range(HALF_STEPS): order_x(t)
         quantise_w(0)
         transpose_r(1)
-        order_w(1)
         transpose_x(0, False, borrow=True)
-        transpose_x(1, True)
+        transpose_x(1, False)
         transpose_x(2, False, borrow=True)
         transpose_x(3, False)
+        order_w(1)
+        transpose_c0()
         quantise_x(0)
         transpose_w(1, on_vector=())
-        transpose_c0()
         order_w(2)
 
         steps = [(jt, first, HALF_STEPS) for jt in range(ROW_TILES - 1) for first in (HALF_STEPS, 0)]
@@ -385,6 +385,8 @@ def tile_lstm_cell_pa_kernel(
                 load_w(jt + LOAD_AHEAD)
             gate_tiles = gates(step)
             before = updated
+            if gated is not None:
+                kept_state(*gated)
             if jt == 0 and opens_row_tile:
                 quantise_w(1)
                 order_w(3)
@@ -396,9 +398,7 @@ def tile_lstm_cell_pa_kernel(
             elif closes_row_tile:
                 pass
             if gated is not None:
-                kept_state(*gated)
-            if gated is not None:
-                updated = (gated[0], new_state(*gated, nc.gpsimd))
+                updated = (gated[0], new_state(*gated, nc.vector if gated[0][:2] == (ROW_TILES - 1, 0) else nc.gpsimd))
             gated = (step, gate_tiles)
             if jt == 0 and opens_row_tile:
                 recurrent_matmuls(1, 0)
@@ -416,7 +416,7 @@ def tile_lstm_cell_pa_kernel(
                 finish(*before)
             if step == (ROW_TILES - 2, 0, HALF_STEPS):
                 store_last(0, WORD_BLOCKS)
-            if step == (ROW_TILES - 1, 6, HALF_STEPS // 2):
+            if step == (ROW_TILES - 1, 0, HALF_STEPS // 2):
                 store_last(WORD_BLOCKS, 3)
         finish(*updated)
         kept_state(*gated)

@@ -111,9 +111,10 @@ def tile_lstm_cell_pa_kernel(
             load_r(jt)
             load_w(jt)
 
-        def order_words(rows_bf16, tag):
-            ordered = order_pool.tile([P, FEATURES], BF16, tag=tag, name="ordered")
-            nc.vector.tensor_copy(
+        def order_words(rows_bf16, on_vector):
+            ordered = order_pool.tile([P, FEATURES], BF16, tag="ordered", name="ordered")
+            leave_psum(
+                on_vector,
                 out=ordered[:].bitcast(F32).rearrange("p (c u s r) -> p c u s r", c=PASSES, u=2, r=RUN),
                 in_=rows_bf16.bitcast(F32).rearrange("p (c s u r) -> p c u s r", c=PASSES, u=2, r=RUN),
             )
@@ -145,8 +146,8 @@ def tile_lstm_cell_pa_kernel(
 
         x_ordered = {}
 
-        def order_x(t):
-            x_ordered[t] = order_words(x_raw[:, t, :], "ordered")
+        def order_x(t, on_vector=True):
+            x_ordered[t] = order_words(x_raw[:, t, :], on_vector)
 
         def transpose_x(t, on_vector, borrow=False):
             bank = transpose_words(x_ordered[t], borrow=borrow)
@@ -164,14 +165,16 @@ def tile_lstm_cell_pa_kernel(
                     in_=x_grouped[:, c, half * 4 * HALF : (half + 1) * 4 * HALF],
                 )
 
-        h0T = const.tile([P, WORD_BLOCKS, BATCH, 2], BF16)
+        h0_words = const.tile([P, WORD_BLOCKS, BATCH, 2], BF16)
+        h0T = const.tile([P, WORD_BLOCKS, 2, BATCH], BF16)
 
         def prepare_h0():
             bank = transpose_words(h0_raw[:])
             nc.vector.tensor_copy(
-                out=h0T[:].rearrange("p q b e -> p (q b e)").bitcast(F32),
+                out=h0_words[:].rearrange("p q b e -> p (q b e)").bitcast(F32),
                 in_=bank[:].rearrange("p q b -> p (q b)"),
             )
+            nc.vector.tensor_copy(out=h0T[:], in_=h0_words[:].rearrange("p q b e -> p q e b"))
 
         r_T = {}
         rec_sums = {}
@@ -206,7 +209,7 @@ def tile_lstm_cell_pa_kernel(
                 nc.tensor.matmul(
                     out=rec_sums[jt][:, n, :],
                     lhsT=r_T[jt][n][:, q, :, e],
-                    rhs=h0T[:, q, :, e],
+                    rhs=h0T[:, q, e, :],
                     start=(q == 0 and e == 0),
                     stop=(q == WORD_BLOCKS - 1 and e == 1),
                 )
@@ -219,9 +222,9 @@ def tile_lstm_cell_pa_kernel(
                     op=ALU.add,
                 )
 
-        def order_w(jt):
+        def order_w(jt, on_scalar=()):
             if jt < ROW_TILES:
-                w_ordered[jt] = [order_words(w_raw[jt][n][:], "ordered") for n in range(GATES)]
+                w_ordered[jt] = [order_words(w_raw[jt][n][:], n not in on_scalar) for n in range(GATES)]
 
         def transpose_w(jt, borrow=False, on_vector=W_ON_VECTOR):
             if jt >= ROW_TILES:
@@ -348,7 +351,10 @@ def tile_lstm_cell_pa_kernel(
         prepare_h0()
         transpose_r(0, borrow=True)
         recurrent_matmuls(0, 0)
-        for t in range(HALF_STEPS, STEPS): order_x(t)
+        order_x(4)
+        order_x(5)
+        order_x(6)
+        order_x(7)
         transpose_x(4, False)
         transpose_x(5, True, borrow=True)
         transpose_x(6, False)
@@ -359,7 +365,10 @@ def tile_lstm_cell_pa_kernel(
         quantise_x(1)
         transpose_w(0, borrow=True, on_vector=(2,))
         recurrent_matmuls(0, 1)
-        for t in range(HALF_STEPS): order_x(t)
+        order_x(0)
+        order_x(1)
+        order_x(2)
+        order_x(3)
         quantise_w(0)
         transpose_r(1)
         transpose_x(0, False, borrow=True)
@@ -418,7 +427,8 @@ def tile_lstm_cell_pa_kernel(
                 store_last(0, WORD_BLOCKS)
             if step == (ROW_TILES - 1, 0, HALF_STEPS // 2):
                 store_last(WORD_BLOCKS, 3)
-        finish(*updated)
         kept_state(*gated)
-        finish(gated[0], new_state(*gated, nc.vector))
+        c_new = new_state(*gated, nc.vector)
+        finish(*updated)
         store_last(ROW_TILES - 1, 1)
+        finish(gated[0], c_new)

from contextlib import ExitStack

import concourse.mybir as mybir
from concourse.masks import make_identity

F32 = mybir.dt.float32
BF16 = mybir.dt.bfloat16
U32 = mybir.dt.uint32
U8 = mybir.dt.uint8
FP8X4 = mybir.dt.float8_e4m3fn_x4
ACT = mybir.ActivationFunctionType
ALU = mybir.AluOpType

P = 128
BATCH, STEPS, FEATURES, HIDDEN = 128, 8, 1024, 1024
GATES = 3
ROW_TILES = HIDDEN // P
WORD_BLOCKS = FEATURES // (2 * P)
PASSES = FEATURES // (4 * P)
HALF_STEPS = STEPS // 2
HALF = HALF_STEPS * BATCH
TOKENS = STEPS * BATCH
RUN = 8
R_ON_VECTOR = ()
W_ON_VECTOR = (0, 1)
LOAD_AHEAD = 4

FLOPS = 2 * TOKENS * FEATURES * HIDDEN * GATES + 2 * BATCH * HIDDEN * HIDDEN * GATES


def tile_lstm_cell_pa_kernel(
    tc, x, h0, c0, W_f, b_f, R_f, rb_f, W_i, b_i, R_i, rb_i, W_g, b_g, R_g, rb_g, out_0, out_1, out_2
):
    nc = tc.nc
    w_dram = (W_f, W_i, W_g)
    r_dram = (R_f, R_i, R_g)
    bias_dram = (b_f, rb_f, b_i, rb_i, b_g, rb_g)

    with ExitStack() as ctx:
        const = ctx.enter_context(tc.tile_pool(name="const", bufs=1))
        raw_pool = ctx.enter_context(tc.tile_pool(name="raw", bufs=2 * GATES * LOAD_AHEAD))
        stage = ctx.enter_context(tc.tile_pool(name="stage", bufs=6))
        order_pool = ctx.enter_context(tc.tile_pool(name="order", bufs=9))
        work = ctx.enter_context(tc.tile_pool(name="work", bufs=4))
        keep = ctx.enter_context(tc.tile_pool(name="keep", bufs=ROW_TILES))
        flip_psum = ctx.enter_context(tc.psum_pool(name="flip_psum", bufs=3))
        rec_psum = ctx.enter_context(tc.psum_pool(name="rec_psum", bufs=1))
        acc_psum = ctx.enter_context(tc.psum_pool(name="acc_psum", bufs=GATES))
        c0_psum = ctx.enter_context(tc.psum_pool(name="c0_psum", bufs=1))

        ctx.enter_context(tc.manual_schedule())

        table_warmer = const.tile([P, 1], F32)
        nc.vector.memset(table_warmer[:], 0.0)
        nc.scalar.activation(out=table_warmer[:], in_=table_warmer[:], func=ACT.Sigmoid)

        ident_f32 = const.tile([P, P], F32)
        make_identity(nc, ident_f32[:])
        ident_bf16 = const.tile([P, P], BF16)
        make_identity(nc, ident_bf16[:])

        bias_rows = const.tile([P, P], BF16)
        nc.vector.memset(bias_rows[:], 0.0)

        x_raw = const.tile([P, STEPS, FEATURES], BF16)
        h0_raw = const.tile([P, HIDDEN], BF16)
        c0_raw = const.tile([P, HIDDEN], BF16)

        def load_x(first_step):
            steps = slice(first_step, first_step + 2)
            nc.sync.dma_start(out=x_raw[:, steps, :], in_=x[:, steps, :])

        def load_rows(matrix, jt, name):
            raw = raw_pool.tile([P, FEATURES], BF16, tag="raw", name=name)
            nc.sync.dma_start(out=raw[:], in_=matrix[jt * P : (jt + 1) * P, :])
            return raw

        def load_r(jt):
            if jt < ROW_TILES:
                r_raw[jt] = [load_rows(r_dram[n], jt, "r_raw") for n in range(GATES)]

        def load_bias(v):
            nc.sync.dma_start(
                out=bias_rows[v * ROW_TILES : (v + 1) * ROW_TILES, :],
                in_=bias_dram[v].rearrange("(jt p) -> jt p", p=P),
            )

        def load_w(jt):
            if jt < ROW_TILES:
                w_raw[jt] = [load_rows(w_dram[n], jt, "w_raw") for n in range(GATES)]

        r_raw = {}
        w_raw = {}
        nc.sync.dma_start(out=h0_raw[:], in_=h0)
        load_r(0)
        load_bias(0)
        load_bias(1)
        load_x(4)
        load_bias(2)
        load_bias(3)
        load_x(6)
        load_bias(4)
        load_bias(5)
        load_w(0)
        load_r(1)
        load_x(0)
        load_x(2)
        nc.sync.dma_start(out=c0_raw[:], in_=c0)
        load_w(1)
        for jt in range(2, LOAD_AHEAD):
            load_r(jt)
            load_w(jt)

        def order_words(rows_bf16, on_vector):
            ordered = order_pool.tile([P, FEATURES], BF16, tag="ordered", name="ordered")
            leave_psum(
                on_vector,
                out=ordered[:].bitcast(F32).rearrange("p (c u s r) -> p c u s r", c=PASSES, u=2, r=RUN),
                in_=rows_bf16.bitcast(F32).rearrange("p (c s u r) -> p c u s r", c=PASSES, u=2, r=RUN),
            )
            return ordered[:]

        def transpose_words(rows_bf16, borrow=False):
            words = rows_bf16.bitcast(F32)
            if borrow:
                bank = acc_psum.tile([P, WORD_BLOCKS, P], F32, tag="acc", name="bank")
            else:
                bank = flip_psum.tile([P, WORD_BLOCKS, P], F32, tag="flip", name="bank")
            for q in range(WORD_BLOCKS):
                nc.tensor.transpose(bank[:, q, :], words[:, q * P : (q + 1) * P], ident_f32[:])
            return bank

        def by_pass(bank):
            return bank[:].rearrange("p (c u) n -> p c n u", u=2)

        def leave_psum(on_vector, out, in_):
            if on_vector:
                nc.vector.tensor_copy(out=out, in_=in_)
            else:
                nc.scalar.copy(out=out, in_=in_)

        x_grouped = const.tile([P, PASSES, 4 * TOKENS], BF16, align_bytes=64)
        x_codes = const.tile([P, PASSES, TOKENS], U32, align_bytes=64)
        x_scales = const.tile([P, PASSES, TOKENS], U8, align_bytes=64)
        x_grouped_words = x_grouped[:].bitcast(F32).rearrange("p c (n u) -> p c n u", u=2)

        x_ordered = {}

        def order_x(t, on_vector=True):
            x_ordered[t] = order_words(x_raw[:, t, :], on_vector)

        def transpose_x(t, on_vector, borrow=False):
            bank = transpose_words(x_ordered[t], borrow=borrow)
            columns = x_grouped_words[:, :, t * BATCH : (t + 1) * BATCH, :]
            if on_vector:
                nc.vector.tensor_copy(out=columns, in_=by_pass(bank))
            else:
                nc.scalar.copy(out=columns, in_=by_pass(bank))

        def quantise_x(half):
            for c in range(PASSES):
                nc.vector.quantize_mx(
                    out=x_codes[:, c, half * HALF : (half + 1) * HALF].bitcast(FP8X4),
                    scales=x_scales[:, c, half * HALF : (half + 1) * HALF],
                    in_=x_grouped[:, c, half * 4 * HALF : (half + 1) * 4 * HALF],
                )

        h0_words = const.tile([P, WORD_BLOCKS, BATCH, 2], BF16)
        h0T = const.tile([P, WORD_BLOCKS, 2, BATCH], BF16)

        def prepare_h0():
            bank = transpose_words(h0_raw[:])
            nc.vector.tensor_copy(
                out=h0_words[:].rearrange("p q b e -> p (q b e)").bitcast(F32),
                in_=bank[:].rearrange("p q b -> p (q b)"),
            )
            nc.vector.tensor_copy(out=h0T[:], in_=h0_words[:].rearrange("p q b e -> p q e b"))

        r_T = {}
        rec_sums = {}
        rec = {}
        w_ordered = {}
        w_grouped = {}
        w_mx = {}

        def transpose_r(jt, borrow=False):
            if jt >= ROW_TILES:
                return
            r_T[jt] = []
            for n in range(GATES):
                bank = transpose_words(r_raw[jt][n][:], borrow=(borrow and n % 2 == 1))
                flipped = stage.tile([P, WORD_BLOCKS, P, 2], BF16, tag="r_T", name="r_T")
                leave_psum(
                    n in R_ON_VECTOR,
                    out=flipped[:].rearrange("p q j e -> p (q j e)").bitcast(F32),
                    in_=bank[:].rearrange("p q j -> p (q j)"),
                )
                r_T[jt].append(flipped)

        rec_steps = [(n, q, e) for n in range(GATES) for q in range(WORD_BLOCKS) for e in range(2)]

        def recurrent_matmuls(jt, part):
            if jt >= ROW_TILES:
                return
            if part == 0:
                rec_sums[jt] = rec_psum.tile([P, GATES, BATCH], F32, tag="rec", name="rec_sums")
            count = len(rec_steps) // 2
            for n, q, e in rec_steps[part * count : (part + 1) * count]:
                nc.tensor.matmul(
                    out=rec_sums[jt][:, n, :],
                    lhsT=r_T[jt][n][:, q, :, e],
                    rhs=h0T[:, q, e, :],
                    start=(q == 0 and e == 0),
                    stop=(q == WORD_BLOCKS - 1 and e == 1),
                )
            if part == 1:
                rec[jt] = work.tile([P, GATES, BATCH], F32, tag="rec_sb", name="rec")
                nc.vector.tensor_tensor(
                    out=rec[jt][:],
                    in0=rec_sums[jt][:],
                    in1=bias[:, :, jt].unsqueeze(2).to_broadcast([P, GATES, BATCH]),
                    op=ALU.add,
                )

        def order_w(jt, on_scalar=()):
            if jt < ROW_TILES:
                w_ordered[jt] = [order_words(w_raw[jt][n][:], n not in on_scalar) for n in range(GATES)]

        def transpose_w(jt, borrow=False, on_vector=W_ON_VECTOR):
            if jt >= ROW_TILES:
                return
            w_grouped[jt] = []
            for n in range(GATES):
                bank = transpose_words(w_ordered[jt][n], borrow=(borrow and n % 2 == 1))
                values = stage.tile([P, 4 * PASSES * P], BF16, tag="w_grouped", name="w_grouped", align_bytes=64)
                leave_psum(
                    n in on_vector,
                    out=values[:].bitcast(F32).rearrange("p (c j u) -> p c j u", c=PASSES, u=2),
                    in_=by_pass(bank),
                )
                w_grouped[jt].append(values)

        def quantise_w(jt):
            if jt >= ROW_TILES:
                return
            w_mx[jt] = []
            for n in range(GATES):
                codes = stage.tile([P, PASSES, P], U32, tag="w_codes", name="w_codes", align_bytes=64)
                scales = stage.tile([P, PASSES, P], U8, tag="w_scales", name="w_scales", align_bytes=64)
                nc.vector.quantize_mx(
                    out=codes[:].rearrange("p c j -> p (c j)").bitcast(FP8X4),
                    scales=scales[:].rearrange("p c j -> p (c j)"),
                    in_=w_grouped[jt][n][:],
                )
                w_mx[jt].append((codes, scales))

        def gates(step):
            jt, first, count = step
            tokens = slice(first * BATCH, (first + count) * BATCH)
            fi = work.tile([P, 2, count, BATCH], F32, tag="fi", name="fi")
            g = work.tile([P, 1, count, BATCH], F32, tag="g", name="g")
            for n in range(GATES):
                codes, scales = w_mx[jt][n]
                acc = acc_psum.tile([P, HALF_STEPS, BATCH], F32, tag="acc", name="acc")
                for c in range(PASSES):
                    nc.tensor.matmul_mx(
                        out=acc[:, 0:count, :].rearrange("p t b -> p (t b)"),
                        lhsT=codes[:, c, :].bitcast(FP8X4),
                        lhsT_scale=scales[:, c, :],
                        rhs=x_codes[:, c, tokens].bitcast(FP8X4),
                        rhs_scale=x_scales[:, c, tokens],
                        start=(c == 0),
                        stop=(c == PASSES - 1),
                    )
                gate = (fi if n < 2 else g)[:, n % 2]
                nc.vector.tensor_tensor(
                    out=gate,
                    in0=acc[:, 0:count, :],
                    in1=rec[jt][:, n, :].unsqueeze(1).to_broadcast([P, count, BATCH]),
                    op=ALU.add,
                )
            nc.scalar.activation(out=fi[:], in_=fi[:], func=ACT.Sigmoid)
            nc.scalar.activation(out=g[:], in_=g[:], func=ACT.Tanh)
            return fi[:, 0], fi[:, 1], g[:, 0]

        def kept_state(step, gate_tiles):
            jt, first, count = step
            f_gate = gate_tiles[0]
            nc.vector.tensor_tensor(
                out=f_gate,
                in0=f_gate,
                in1=c0T[:, jt, :].unsqueeze(1).to_broadcast([P, count, BATCH]),
                op=ALU.mult,
            )

        def has_last_time_step(step):
            return step[1] + step[2] == STEPS

        def new_state(step, gate_tiles, engine):
            f_gate, i_gate, g_gate = gate_tiles
            engine.tensor_tensor(out=i_gate, in0=i_gate, in1=g_gate, op=ALU.mult)
            pool = keep if has_last_time_step(step) else work
            c_new = pool.tile([P, step[2], BATCH], F32, tag="c_new", name="c_new")
            engine.tensor_tensor(out=c_new[:], in0=f_gate, in1=i_gate, op=ALU.add)
            return c_new

        def finish(step, c_new):
            jt, first, count = step
            pool = keep if has_last_time_step(step) else work
            h_new = pool.tile([P, count, BATCH], F32, tag="h_new", name="h_new")
            nc.scalar.activation(out=h_new[:], in_=c_new[:], func=ACT.Tanh)
            nc.sync.dma_start(
                out=out_0[jt * P : (jt + 1) * P, first * BATCH : (first + count) * BATCH],
                in_=h_new[:].rearrange("p t b -> p (t b)"),
            )
            if has_last_time_step(step):
                last_tiles[jt] = (h_new[:, count - 1, :], c_new[:, count - 1, :])

        last_tiles = {}
        last_sb = const.tile([P, 2, HIDDEN], F32)

        def store_last(first, count):
            columns = slice(first * P, (first + count) * P)
            for which, out_last in enumerate((out_1, out_2)):
                bank = flip_psum.tile([P, WORD_BLOCKS, P], F32, tag="flip", name="last_bank")
                for q in range(count):
                    nc.tensor.transpose(bank[:, q, :], last_tiles[first + q][which], ident_f32[:])
                leave_psum(which == 1, out=last_sb[:, which, columns], in_=bank[:, 0:count, :].rearrange("p q j -> p (q j)"))
                nc.sync.dma_start(out=out_last[:, columns], in_=last_sb[:, which, columns])

        bias_pairs = const.tile([P, GATES, 2, ROW_TILES], F32)
        bias = const.tile([P, GATES, ROW_TILES], F32)
        c0T = c0_psum.tile([P, ROW_TILES, BATCH], BF16, tag="c0T", name="c0T")

        def prepare_bias():
            bias_psum = flip_psum.tile([P, P], BF16, tag="flip", name="bias_psum")
            nc.tensor.transpose(bias_psum[:], bias_rows[:], ident_bf16[:])
            nc.vector.tensor_copy(
                out=bias_pairs[:],
                in_=bias_psum[:, 0 : 2 * GATES * ROW_TILES].rearrange("p (n s jt) -> p n s jt", n=GATES, s=2),
            )

        def add_bias():
            nc.vector.tensor_tensor(out=bias[:], in0=bias_pairs[:, :, 0, :], in1=bias_pairs[:, :, 1, :], op=ALU.add)

        def transpose_c0():
            for tile in range(ROW_TILES):
                nc.tensor.transpose(c0T[:, tile, :], c0_raw[:, tile * P : (tile + 1) * P], ident_bf16[:])


        prepare_h0()
        transpose_r(0, borrow=True)
        recurrent_matmuls(0, 0)
        order_x(4)
        order_x(5)
        order_x(6)
        order_x(7)
        transpose_x(4, False)
        transpose_x(5, True, borrow=True)
        transpose_x(6, False)
        transpose_x(7, False, borrow=True)
        order_w(0)
        prepare_bias()
        add_bias()
        quantise_x(1)
        transpose_w(0, borrow=True, on_vector=(2,))
        recurrent_matmuls(0, 1)
        order_x(0)
        order_x(1)
        order_x(2)
        order_x(3)
        quantise_w(0)
        transpose_r(1)
        transpose_x(0, False, borrow=True)
        transpose_x(1, False)
        transpose_x(2, False, borrow=True)
        transpose_x(3, False)
        order_w(1)
        transpose_c0()
        quantise_x(0)
        transpose_w(1, on_vector=())
        order_w(2)

        steps = [(jt, first, HALF_STEPS) for jt in range(ROW_TILES - 1) for first in (HALF_STEPS, 0)]
        steps += [(ROW_TILES - 1, first, HALF_STEPS // 2) for first in (4, 6, 0, 2)]
        gated = None
        updated = None
        for step in steps:
            jt, first, count = step
            opens_row_tile = first == HALF_STEPS
            closes_row_tile = first == 0
            if opens_row_tile:
                load_r(jt + LOAD_AHEAD)
                load_w(jt + LOAD_AHEAD)
            gate_tiles = gates(step)
            before = updated
            if gated is not None:
                kept_state(*gated)
            if jt == 0 and opens_row_tile:
                quantise_w(1)
                order_w(3)
            elif jt == 0:
                pass
            elif opens_row_tile:
                quantise_w(jt + 1)
                order_w(jt + 3)
            elif closes_row_tile:
                pass
            if gated is not None:
                updated = (gated[0], new_state(*gated, nc.vector if gated[0][:2] == (ROW_TILES - 1, 0) else nc.gpsimd))
            gated = (step, gate_tiles)
            if jt == 0 and opens_row_tile:
                recurrent_matmuls(1, 0)
                transpose_r(2)
            elif jt == 0:
                recurrent_matmuls(1, 1)
                transpose_w(2)
            elif opens_row_tile:
                recurrent_matmuls(jt + 1, 0)
                transpose_r(jt + 2)
            elif closes_row_tile:
                recurrent_matmuls(jt + 1, 1)
                transpose_w(jt + 2)
            if before is not None:
                finish(*before)
            if step == (ROW_TILES - 2, 0, HALF_STEPS):
                store_last(0, WORD_BLOCKS)
            if step == (ROW_TILES - 1, 0, HALF_STEPS // 2):
                store_last(WORD_BLOCKS, 3)
        kept_state(*gated)
        c_new = new_state(*gated, nc.vector)
        finish(*updated)
        store_last(ROW_TILES - 1, 1)
        finish(gated[0], c_new)
